import numpy as np
import ml_dtypes


def mxq(x, axis, fmt="e4m3"):
    dtype, down = {"e4m3": (ml_dtypes.float8_e4m3fn, 7), "e5m2": (ml_dtypes.float8_e5m2, 14)}[fmt]
    v = np.moveaxis(np.asarray(x, np.float32).astype(ml_dtypes.bfloat16).astype(np.float64), axis, -1)
    blocks = v.reshape(v.shape[:-1] + (-1, 32))
    amax = np.abs(blocks).max(-1, keepdims=True)
    byte = np.maximum(np.where(amax > 0, np.frexp(amax)[1] - 1 + 127, 0) - down, 1)
    scale = np.exp2(byte - 127.0)
    codes = (blocks / scale).astype(np.float32).astype(dtype).astype(np.float64)
    return np.moveaxis((codes * scale).reshape(v.shape), -1, axis)


WIDE = False


def mx_kscale(k):
    if not WIDE:
        return np.ones(k)
    levels = np.array([10, -10, 5, -5, 0])
    a = np.random.permutation(np.resize(levels, k // 512 * 4)).reshape(k // 512, 4)
    idx = np.arange(k)
    return np.exp2(a[idx // 512, idx % 128 // 32])


BF16 = ml_dtypes.bfloat16


def bf(x):
    return np.asarray(x, np.float32).astype(BF16)


def f64(x):
    return np.asarray(x).astype(np.float64)


E2M1 = np.array([0.0, 0.5, 1.0, 1.5, 2.0, 3.0, 4.0, 6.0, -0.0, -0.5, -1.0, -1.5, -2.0, -3.0, -4.0, -6.0])


def pack_weight(w, fmt):
    k, n = w.shape
    w = f64(bf(w)).reshape(k // 32, 32, n)
    amax = np.abs(w).max(1)
    if fmt == "e4m3":
        byte = np.frexp(amax)[1] - 1 + 127 - 7
    else:
        mant, ex = np.frexp(amax / 6.0)
        byte = np.where(mant > 0.5, ex, ex - 1) + 127
    byte = np.clip(np.where(amax > 0, byte, 1), 1, 254)
    scaled = (w * np.exp2(127.0 - byte)[:, None, :]).reshape(k, n).astype(np.float32)
    by_word = np.ascontiguousarray(scaled.reshape(k // 512, 128, 4, n).transpose(0, 1, 3, 2))
    if fmt == "e4m3":
        words = by_word.astype(ml_dtypes.float8_e4m3fn).view(np.uint8)
    else:
        c = by_word.astype(ml_dtypes.float4_e2m1fn).view(np.uint8) & 0xF
        words = c[..., 0::2] | (c[..., 1::2] << 4)
    return np.ascontiguousarray(words), np.ascontiguousarray(byte.astype(np.uint8).reshape(k // 512, 16, n))


def unpack_weight(words, scales, fmt):
    g, p, n, _ = words.shape
    if fmt == "e4m3":
        vals = np.ascontiguousarray(words).view(ml_dtypes.float8_e4m3fn).astype(np.float64)
    else:
        nib = np.empty((g, p, n, 4), np.uint8)
        nib[..., 0::2] = words & 0xF
        nib[..., 1::2] = words >> 4
        vals = E2M1[nib]
    vals = vals * np.repeat(np.exp2(scales.astype(np.float64) - 127.0), 8, axis=1)[..., None]
    return vals.transpose(0, 1, 3, 2).reshape(g * 512, n)


B, HID, UD = 4096, 512, 512
FMT = "e4m3"


def sigmoid(v):
    return 1.0 / (1.0 + np.exp(-v))


def setup_inputs():
    s, u = mx_kscale(HID), mx_kscale(UD)
    encoder_hidden = bf(np.random.standard_normal((B, HID)) * s)
    spk_vectors = bf(np.random.standard_normal((B, UD)))
    adr_vectors = bf(np.random.standard_normal((B, UD)) * u)
    h_tilde = bf(np.tanh(np.random.standard_normal((B, UD)) * 1.3))
    xz_words, xz_scales = pack_weight((np.random.standard_normal((UD, HID)) / np.sqrt(HID) / s).T, FMT)
    hz_words, hz_scales = pack_weight((np.random.standard_normal((UD, UD)) / np.sqrt(UD)).T, FMT)
    vz_words, vz_scales = pack_weight((np.random.standard_normal((UD, UD)) / np.sqrt(UD) / u).T, FMT)
    return {
        "encoder_hidden": encoder_hidden,
        "spk_vectors": spk_vectors,
        "adr_vectors": adr_vectors,
        "h_tilde": h_tilde,
        "WA_xz_words": xz_words,
        "WA_xz_scales": xz_scales,
        "WA_hz_words": hz_words,
        "WA_hz_scales": hz_scales,
        "VA_hz_words": vz_words,
        "VA_hz_scales": vz_scales,
    }


def reference(encoder_hidden, spk_vectors, adr_vectors, h_tilde, WA_xz_words, WA_xz_scales,
              WA_hz_words, WA_hz_scales, VA_hz_words, VA_hz_scales):
    x, hs, ha = f64(encoder_hidden), f64(spk_vectors), f64(adr_vectors)
    z_t = sigmoid((mxq(x, 1, "e4m3") @ unpack_weight(WA_xz_words, WA_xz_scales, FMT))
                  + (mxq(hs, 1, "e4m3") @ unpack_weight(WA_hz_words, WA_hz_scales, FMT))
                  + (mxq(ha, 1, "e4m3") @ unpack_weight(VA_hz_words, VA_hz_scales, FMT)))
    return (1.0 - z_t) * hs + z_t * f64(h_tilde)

@@ -1,0 +1,179 @@
+from contextlib import ExitStack
+
+import concourse.mybir as mybir
+from concourse.masks import make_identity
+
+F32 = mybir.dt.float32
+BF16 = mybir.dt.bfloat16
+I32 = mybir.dt.int32
+U32 = mybir.dt.uint32
+U8 = mybir.dt.uint8
+FP8X4 = mybir.dt.float8_e4m3fn_x4
+ALU = mybir.AluOpType
+ACT = mybir.ActivationFunctionType
+
+P = 128
+PACK = 4
+HALVES = 2
+ROWS = 4096
+K = 512
+N = 512
+N_TILES = ROWS // P
+PAIR = 2
+N_PAIRS = N_TILES // PAIR
+QUANTISED = ("x", "hs", "ha")
+LOADED = QUANTISED + ("ht",)
+SCALE_ROWS = 4
+QUADRANT = 32
+
+LOAD_AHEAD = 4
+MX_LAG = 1
+DIFF_AHEAD = 1
+
+FLOPS = 2 * ROWS * K * N * len(QUANTISED)
+
+
+def tile_updatespeaker_pc_t_kernel(
+    tc,
+    encoder_hidden,
+    spk_vectors,
+    adr_vectors,
+    h_tilde,
+    WA_xz_words,
+    WA_xz_scales,
+    WA_hz_words,
+    WA_hz_scales,
+    VA_hz_words,
+    VA_hz_scales,
+    out,
+):
+    nc = tc.nc
+    by_tile = "(p j) c -> p j c"
+    sources = {
+        "x": encoder_hidden.rearrange(by_tile, j=N_TILES),
+        "hs": spk_vectors.rearrange(by_tile, j=N_TILES),
+        "ha": adr_vectors.rearrange(by_tile, j=N_TILES),
+        "ht": h_tilde.rearrange(by_tile, j=N_TILES),
+    }
+    out_tiles = out.rearrange(by_tile, j=N_TILES)
+    weight_words = (WA_xz_words, WA_hz_words, VA_hz_words)
+    weight_scales = (WA_xz_scales, WA_hz_scales, VA_hz_scales)
+
+    with ExitStack() as ctx:
+        consts = ctx.enter_context(tc.tile_pool(name="consts", bufs=1))
+        inputs = ctx.enter_context(tc.tile_pool(name="inputs", bufs=N_PAIRS))
+        grouped_pool = ctx.enter_context(tc.tile_pool(name="grouped", bufs=3))
+        code_pool = ctx.enter_context(tc.tile_pool(name="codes", bufs=3))
+        gate_pool = ctx.enter_context(tc.tile_pool(name="gate", bufs=3))
+        blend_pool = ctx.enter_context(tc.tile_pool(name="blend", bufs=5))
+        planes_psum = ctx.enter_context(tc.psum_pool(name="planes", bufs=2))
+        sums_psum = ctx.enter_context(tc.psum_pool(name="sums", bufs=4))
+        ctx.enter_context(tc.manual_schedule())
+
+        loaded = {}
+        grouped = {}
+        codes = {}
+        scales = {}
+        gate = {}
+        blend = {}
+
+        def load_pair(a):
+            for name in LOADED:
+                loaded[(name, a)] = inputs.tile([P, PAIR, K], BF16, name="%s_%d" % (name, a), tag=name)
+                nc.sync.dma_start(out=loaded[(name, a)][:], in_=sources[name][:, PAIR * a : PAIR * (a + 1), :])
+
+        def transpose_tile(a, s):
+            if s == 0:
+                grouped[a] = grouped_pool.tile(
+                    [P, len(QUANTISED), PAIR, P, PACK], BF16, name="grouped_%d" % a, tag="grouped", align_bytes=64
+                )
+            two = planes_psum.tile([P, 2, HALVES, P], F32, name="two_%d_%d" % (a, s), tag="two")
+            one = planes_psum.tile([P, 1, HALVES, P], F32, name="one_%d_%d" % (a, s), tag="one")
+            for i, name in enumerate(QUANTISED):
+                words = loaded[(name, a)][:, s, :].bitcast(F32)
+                bank = two[:, i] if i < 2 else one[:, 0]
+                for u in range(HALVES):
+                    nc.tensor.transpose(bank[:, u, :], words[:, u : K // 2 : HALVES], identity[:])
+            as_words = grouped[a][:].bitcast(F32)
+            nc.scalar.copy(out=as_words[:, 0:2, s], in_=two[:].rearrange("p i u r -> p i r u"))
+            nc.scalar.copy(out=as_words[:, 2:3, s], in_=one[:].rearrange("p i u r -> p i r u"))
+
+        def quantise_pair(a):
+            codes[a] = code_pool.tile([P, len(QUANTISED), PAIR * P], U32, name="codes_%d" % a, tag="codes", align_bytes=64)
+            scales[a] = code_pool.tile([P, len(QUANTISED), PAIR * P], U8, name="scales_%d" % a, tag="scales", align_bytes=64)
+            for i in range(len(QUANTISED)):
+                nc.vector.quantize_mx(
+                    out=codes[a][:, i, :].bitcast(FP8X4),
+                    scales=scales[a][:, i, :],
+                    in_=grouped[a][:, i].rearrange("p s r t -> p (s r t)"),
+                )
+
+        def multiply_tile(a, s):
+            if s == 0:
+                gate[a] = gate_pool.tile([P, PAIR, N], F32, name="gate_%d" % a, tag="gate")
+            rows = slice(s * P, (s + 1) * P)
+            sums = sums_psum.tile([P, N], F32, name="sums_%d_%d" % (a, s), tag="sums")
+            for i in range(len(QUANTISED)):
+                nc.tensor.matmul_mx(
+                    out=sums[:],
+                    lhsT=codes[a][:, i, rows].bitcast(FP8X4),
+                    lhsT_scale=scales[a][:, i, rows],
+                    rhs=w_words[:, i, :].bitcast(FP8X4),
+                    rhs_scale=w_scales[:, i, :],
+                    start=(i == 0),
+                    stop=(i == len(QUANTISED) - 1),
+                )
+            nc.scalar.activation(out=gate[a][:, s, :], in_=sums[:], func=ACT.Sigmoid)
+
+        def difference(a):
+            blend[a] = blend_pool.tile([P, PAIR, N], F32, name="blend_%d" % a, tag="blend")
+            nc.vector.tensor_tensor(out=blend[a][:], in0=loaded[("ht", a)][:], in1=loaded[("hs", a)][:], op=ALU.subtract)
+
+        def finish_pair(a):
+            for s in range(PAIR):
+                nc.vector.tensor_tensor(out=blend[a][:, s, :], in0=blend[a][:, s, :], in1=gate[a][:, s, :], op=ALU.mult)
+            for s in range(PAIR):
+                nc.vector.tensor_tensor(out=blend[a][:, s, :], in0=blend[a][:, s, :], in1=loaded[("hs", a)][:, s, :], op=ALU.add)
+            nc.sync.dma_start(out=out_tiles[:, PAIR * a : PAIR * (a + 1), :], in_=blend[a][:])
+
+        w_words = consts.tile([P, len(QUANTISED), N], U32, align_bytes=64)
+        w_scales = consts.tile([P, len(QUANTISED), N], U8, align_bytes=64)
+        identity = consts.tile([P, P], F32)
+        warm = consts.tile([P, 1], F32)
+        nc.vector.memset(w_scales[:].bitcast(I32), 0)
+        nc.vector.memset(warm[:], 0.0)
+        nc.scalar.activation(out=warm[:], in_=warm[:], func=ACT.Sigmoid)
+        make_identity(nc, identity[:])
+
+        load_pair(0)
+        for i in range(len(QUANTISED)):
+            for q in range(P // QUADRANT):
+                nc.sync.dma_start(
+                    out=w_scales[QUADRANT * q : QUADRANT * q + SCALE_ROWS, i, :].bitcast(I32),
+                    in_=weight_scales[i][0, SCALE_ROWS * q : SCALE_ROWS * (q + 1), :].bitcast(I32),
+                )
+        load_pair(1)
+        for i in range(len(QUANTISED)):
+            nc.sync.dma_start(
+                out=w_words[:, i, :].bitcast(I32),
+                in_=weight_words[i][0].rearrange("p n t -> p (n t)").bitcast(I32),
+            )
+        for a in range(2, LOAD_AHEAD):
+            load_pair(a)
+        for a in range(DIFF_AHEAD):
+            difference(a)
+
+        for a in range(N_PAIRS + MX_LAG):
+            if a + LOAD_AHEAD < N_PAIRS:
+                load_pair(a + LOAD_AHEAD)
+            for s in range(PAIR):
+                if a < N_PAIRS:
+                    transpose_tile(a, s)
+                if a >= MX_LAG:
+                    multiply_tile(a - MX_LAG, s)
+            if a < N_PAIRS:
+                quantise_pair(a)
+            if a + DIFF_AHEAD < N_PAIRS:
+                difference(a + DIFF_AHEAD)
+            if a >= MX_LAG:
+                finish_pair(a - MX_LAG)

@@ -27,8 +27,8 @@ SCALE_ROWS = 4
 QUADRANT = 32
 
 LOAD_AHEAD = 4
-MX_LAG = 1
-DIFF_AHEAD = 1
+MX_LAG = 3
+BLEND_LAG = 4
 
 FLOPS = 2 * ROWS * K * N * len(QUANTISED)
 
@@ -63,9 +63,9 @@ def tile_updatespeaker_pc_t_kernel(
         consts = ctx.enter_context(tc.tile_pool(name="consts", bufs=1))
         inputs = ctx.enter_context(tc.tile_pool(name="inputs", bufs=N_PAIRS))
         grouped_pool = ctx.enter_context(tc.tile_pool(name="grouped", bufs=3))
-        code_pool = ctx.enter_context(tc.tile_pool(name="codes", bufs=3))
-        gate_pool = ctx.enter_context(tc.tile_pool(name="gate", bufs=3))
-        blend_pool = ctx.enter_context(tc.tile_pool(name="blend", bufs=5))
+        code_pool = ctx.enter_context(tc.tile_pool(name="codes", bufs=4))
+        gate_pool = ctx.enter_context(tc.tile_pool(name="gate", bufs=4))
+        blend_pool = ctx.enter_context(tc.tile_pool(name="blend", bufs=6))
         planes_psum = ctx.enter_context(tc.psum_pool(name="planes", bufs=2))
         sums_psum = ctx.enter_context(tc.psum_pool(name="sums", bufs=4))
         ctx.enter_context(tc.manual_schedule())
@@ -82,13 +82,27 @@ def tile_updatespeaker_pc_t_kernel(
                 loaded[(name, a)] = inputs.tile([P, PAIR, K], BF16, name="%s_%d" % (name, a), tag=name)
                 nc.sync.dma_start(out=loaded[(name, a)][:], in_=sources[name][:, PAIR * a : PAIR * (a + 1), :])
 
-        def transpose_tile(a, s):
+        def load_weight_scales(i):
+            for q in range(P // QUADRANT):
+                nc.sync.dma_start(
+                    out=w_scales[QUADRANT * q : QUADRANT * q + SCALE_ROWS, i, :].bitcast(I32),
+                    in_=weight_scales[i][0, SCALE_ROWS * q : SCALE_ROWS * (q + 1), :].bitcast(I32),
+                )
+
+        def load_weight_words(i):
+            nc.sync.dma_start(
+                out=w_words[:, i, :].bitcast(I32),
+                in_=weight_words[i][0].rearrange("p n t -> p (n t)").bitcast(I32),
+            )
+
+        def transpose_tile(j):
+            a, s = divmod(j, PAIR)
             if s == 0:
                 grouped[a] = grouped_pool.tile(
                     [P, len(QUANTISED), PAIR, P, PACK], BF16, name="grouped_%d" % a, tag="grouped", align_bytes=64
                 )
-            two = planes_psum.tile([P, 2, HALVES, P], F32, name="two_%d_%d" % (a, s), tag="two")
-            one = planes_psum.tile([P, 1, HALVES, P], F32, name="one_%d_%d" % (a, s), tag="one")
+            two = planes_psum.tile([P, 2, HALVES, P], F32, name="two_%d" % j, tag="two")
+            one = planes_psum.tile([P, 1, HALVES, P], F32, name="one_%d" % j, tag="one")
             for i, name in enumerate(QUANTISED):
                 words = loaded[(name, a)][:, s, :].bitcast(F32)
                 bank = two[:, i] if i < 2 else one[:, 0]
@@ -101,18 +115,19 @@ def tile_updatespeaker_pc_t_kernel(
         def quantise_pair(a):
             codes[a] = code_pool.tile([P, len(QUANTISED), PAIR * P], U32, name="codes_%d" % a, tag="codes", align_bytes=64)
             scales[a] = code_pool.tile([P, len(QUANTISED), PAIR * P], U8, name="scales_%d" % a, tag="scales", align_bytes=64)
-            for i in range(len(QUANTISED)):
+            for some in (slice(0, 2), slice(2, 3)):
                 nc.vector.quantize_mx(
-                    out=codes[a][:, i, :].bitcast(FP8X4),
-                    scales=scales[a][:, i, :],
-                    in_=grouped[a][:, i].rearrange("p s r t -> p (s r t)"),
+                    out=codes[a][:, some, :].rearrange("p i w -> p (i w)").bitcast(FP8X4),
+                    scales=scales[a][:, some, :].rearrange("p i w -> p (i w)"),
+                    in_=grouped[a][:, some].rearrange("p i s r t -> p (i s r t)"),
                 )
 
-        def multiply_tile(a, s):
+        def multiply_tile(j):
+            a, s = divmod(j, PAIR)
             if s == 0:
                 gate[a] = gate_pool.tile([P, PAIR, N], F32, name="gate_%d" % a, tag="gate")
             rows = slice(s * P, (s + 1) * P)
-            sums = sums_psum.tile([P, N], F32, name="sums_%d_%d" % (a, s), tag="sums")
+            sums = sums_psum.tile([P, N], F32, name="sums_%d" % j, tag="sums")
             for i in range(len(QUANTISED)):
                 nc.tensor.matmul_mx(
                     out=sums[:],
@@ -129,12 +144,14 @@ def tile_updatespeaker_pc_t_kernel(
             blend[a] = blend_pool.tile([P, PAIR, N], F32, name="blend_%d" % a, tag="blend")
             nc.vector.tensor_tensor(out=blend[a][:], in0=loaded[("ht", a)][:], in1=loaded[("hs", a)][:], op=ALU.subtract)
 
-        def finish_pair(a):
-            for s in range(PAIR):
-                nc.vector.tensor_tensor(out=blend[a][:, s, :], in0=blend[a][:, s, :], in1=gate[a][:, s, :], op=ALU.mult)
-            for s in range(PAIR):
-                nc.vector.tensor_tensor(out=blend[a][:, s, :], in0=blend[a][:, s, :], in1=loaded[("hs", a)][:, s, :], op=ALU.add)
-            nc.sync.dma_start(out=out_tiles[:, PAIR * a : PAIR * (a + 1), :], in_=blend[a][:])
+        def apply_gate(j):
+            a, s = divmod(j, PAIR)
+            nc.vector.tensor_tensor(out=blend[a][:, s, :], in0=blend[a][:, s, :], in1=gate[a][:, s, :], op=ALU.mult)
+
+        def add_speaker_and_store(j):
+            a, s = divmod(j, PAIR)
+            nc.vector.tensor_tensor(out=blend[a][:, s, :], in0=blend[a][:, s, :], in1=loaded[("hs", a)][:, s, :], op=ALU.add)
+            nc.sync.dma_start(out=out_tiles[:, j, :], in_=blend[a][:, s, :])
 
         w_words = consts.tile([P, len(QUANTISED), N], U32, align_bytes=64)
         w_scales = consts.tile([P, len(QUANTISED), N], U8, align_bytes=64)
@@ -146,34 +163,28 @@ def tile_updatespeaker_pc_t_kernel(
         make_identity(nc, identity[:])
 
         load_pair(0)
-        for i in range(len(QUANTISED)):
-            for q in range(P // QUADRANT):
-                nc.sync.dma_start(
-                    out=w_scales[QUADRANT * q : QUADRANT * q + SCALE_ROWS, i, :].bitcast(I32),
-                    in_=weight_scales[i][0, SCALE_ROWS * q : SCALE_ROWS * (q + 1), :].bitcast(I32),
-                )
+        load_weight_scales(0)
         load_pair(1)
+        load_weight_scales(1)
         for i in range(len(QUANTISED)):
-            nc.sync.dma_start(
-                out=w_words[:, i, :].bitcast(I32),
-                in_=weight_words[i][0].rearrange("p n t -> p (n t)").bitcast(I32),
-            )
+            load_weight_words(i)
+        load_weight_scales(2)
         for a in range(2, LOAD_AHEAD):
             load_pair(a)
-        for a in range(DIFF_AHEAD):
-            difference(a)
 
-        for a in range(N_PAIRS + MX_LAG):
-            if a + LOAD_AHEAD < N_PAIRS:
+        for j in range(N_TILES + BLEND_LAG):
+            a, s = divmod(j, PAIR)
+            if s == 0 and a + LOAD_AHEAD < N_PAIRS:
                 load_pair(a + LOAD_AHEAD)
-            for s in range(PAIR):
-                if a < N_PAIRS:
-                    transpose_tile(a, s)
-                if a >= MX_LAG:
-                    multiply_tile(a - MX_LAG, s)
-            if a < N_PAIRS:
+            if j < N_TILES:
+                transpose_tile(j)
+            if MX_LAG <= j < N_TILES + MX_LAG:
+                multiply_tile(j - MX_LAG)
+            if j >= BLEND_LAG:
+                apply_gate(j - BLEND_LAG)
+            if j < N_TILES and s == 0:
+                difference(a)
+            if j < N_TILES and s == 1:
                 quantise_pair(a)
-            if a + DIFF_AHEAD < N_PAIRS:
-                difference(a + DIFF_AHEAD)
-            if a >= MX_LAG:
-                finish_pair(a - MX_LAG)
+            if j >= BLEND_LAG:
+                add_speaker_and_store(j - BLEND_LAG)

@@ -29,6 +29,7 @@ QUADRANT = 32
 LOAD_AHEAD = 4
 MX_LAG = 3
 BLEND_LAG = 4
+TENSOR_SHARE = 4
 
 FLOPS = 2 * ROWS * K * N * len(QUANTISED)
 
@@ -67,7 +68,8 @@ def tile_updatespeaker_pc_t_kernel(
         gate_pool = ctx.enter_context(tc.tile_pool(name="gate", bufs=4))
         blend_pool = ctx.enter_context(tc.tile_pool(name="blend", bufs=6))
         planes_psum = ctx.enter_context(tc.psum_pool(name="planes", bufs=2))
-        sums_psum = ctx.enter_context(tc.psum_pool(name="sums", bufs=4))
+        sums_psum = ctx.enter_context(tc.psum_pool(name="sums", bufs=3))
+        diff_psum = ctx.enter_context(tc.psum_pool(name="diff", bufs=1))
         ctx.enter_context(tc.manual_schedule())
 
         loaded = {}
@@ -76,6 +78,7 @@ def tile_updatespeaker_pc_t_kernel(
         scales = {}
         gate = {}
         blend = {}
+        diff = {}
 
         def load_pair(a):
             for name in LOADED:
@@ -139,14 +142,31 @@ def tile_updatespeaker_pc_t_kernel(
                     stop=(i == len(QUANTISED) - 1),
                 )
             nc.scalar.activation(out=gate[a][:, s, :], in_=sums[:], func=ACT.Sigmoid)
+            if by_tensor(j):
+                diff[j] = diff_psum.tile([P, N], F32, name="diff_%d" % j, tag="diff")
+                nc.tensor.matmul(out=diff[j][:], lhsT=plus_identity[:], rhs=loaded[("ht", a)][:, s, :], start=True, stop=False)
+                nc.tensor.matmul(out=diff[j][:], lhsT=minus_identity[:], rhs=loaded[("hs", a)][:, s, :], start=False, stop=True)
 
-        def difference(a):
-            blend[a] = blend_pool.tile([P, PAIR, N], F32, name="blend_%d" % a, tag="blend")
-            nc.vector.tensor_tensor(out=blend[a][:], in0=loaded[("ht", a)][:], in1=loaded[("hs", a)][:], op=ALU.subtract)
+        def by_tensor(j):
+            return j % TENSOR_SHARE == TENSOR_SHARE - 1
+
+        def difference(j):
+            a, s = divmod(j, PAIR)
+            if s == 0:
+                blend[a] = blend_pool.tile([P, PAIR, N], F32, name="blend_%d" % a, tag="blend")
+            if not by_tensor(j):
+                nc.vector.tensor_tensor(
+                    out=blend[a][:, s, :], in0=loaded[("ht", a)][:, s, :], in1=loaded[("hs", a)][:, s, :], op=ALU.subtract
+                )
 
         def apply_gate(j):
             a, s = divmod(j, PAIR)
-            nc.vector.tensor_tensor(out=blend[a][:, s, :], in0=blend[a][:, s, :], in1=gate[a][:, s, :], op=ALU.mult)
+            nc.vector.tensor_tensor(
+                out=blend[a][:, s, :],
+                in0=diff[j][:] if by_tensor(j) else blend[a][:, s, :],
+                in1=gate[a][:, s, :],
+                op=ALU.mult,
+            )
 
         def add_speaker_and_store(j):
             a, s = divmod(j, PAIR)
@@ -161,6 +181,10 @@ def tile_updatespeaker_pc_t_kernel(
         nc.vector.memset(warm[:], 0.0)
         nc.scalar.activation(out=warm[:], in_=warm[:], func=ACT.Sigmoid)
         make_identity(nc, identity[:])
+        plus_identity = consts.tile([P, P], BF16)
+        minus_identity = consts.tile([P, P], BF16)
+        make_identity(nc, plus_identity[:])
+        nc.vector.tensor_scalar_mul(out=minus_identity[:], in0=plus_identity[:], scalar1=-1.0)
 
         load_pair(0)
         load_weight_scales(0)
@@ -182,8 +206,8 @@ def tile_updatespeaker_pc_t_kernel(
                 multiply_tile(j - MX_LAG)
             if j >= BLEND_LAG:
                 apply_gate(j - BLEND_LAG)
-            if j < N_TILES and s == 0:
-                difference(a)
+            if j < N_TILES:
+                difference(j)
             if j < N_TILES and s == 1:
                 quantise_pair(a)
             if j >= BLEND_LAG:

@@ -70,7 +70,6 @@ def tile_updatespeaker_pc_t_kernel(
         planes_psum = ctx.enter_context(tc.psum_pool(name="planes", bufs=2))
         sums_psum = ctx.enter_context(tc.psum_pool(name="sums", bufs=3))
         diff_psum = ctx.enter_context(tc.psum_pool(name="diff", bufs=1))
-        ctx.enter_context(tc.manual_schedule())
 
         loaded = {}
         grouped = {}

@@ -22,14 +22,15 @@ N_TILES = ROWS // P
 PAIR = 2
 N_PAIRS = N_TILES // PAIR
 QUANTISED = ("x", "hs", "ha")
-LOADED = QUANTISED + ("ht",)
+LOADED = ("hs", "x", "ha", "ht")
 SCALE_ROWS = 4
 QUADRANT = 32
 
 LOAD_AHEAD = 4
-MX_LAG = 3
-BLEND_LAG = 4
-TENSOR_SHARE = 4
+MX_LAG = 1
+BLEND_LAG = 2
+TENSOR_TILES = (1, 3, 5)
+TENSOR_PERIOD = 8
 
 FLOPS = 2 * ROWS * K * N * len(QUANTISED)
 
@@ -61,15 +62,16 @@ def tile_updatespeaker_pc_t_kernel(
     weight_scales = (WA_xz_scales, WA_hz_scales, VA_hz_scales)
 
     with ExitStack() as ctx:
+        ctx.enter_context(tc.manual_schedule())
         consts = ctx.enter_context(tc.tile_pool(name="consts", bufs=1))
         inputs = ctx.enter_context(tc.tile_pool(name="inputs", bufs=N_PAIRS))
         grouped_pool = ctx.enter_context(tc.tile_pool(name="grouped", bufs=3))
-        code_pool = ctx.enter_context(tc.tile_pool(name="codes", bufs=4))
-        gate_pool = ctx.enter_context(tc.tile_pool(name="gate", bufs=4))
+        code_pool = ctx.enter_context(tc.tile_pool(name="codes", bufs=3))
+        gate_pool = ctx.enter_context(tc.tile_pool(name="gate", bufs=3))
         blend_pool = ctx.enter_context(tc.tile_pool(name="blend", bufs=6))
-        planes_psum = ctx.enter_context(tc.psum_pool(name="planes", bufs=2))
-        sums_psum = ctx.enter_context(tc.psum_pool(name="sums", bufs=3))
-        diff_psum = ctx.enter_context(tc.psum_pool(name="diff", bufs=1))
+        planes_psum = ctx.enter_context(tc.psum_pool(name="planes", bufs=4))
+        sums_psum = ctx.enter_context(tc.psum_pool(name="sums", bufs=2))
+        diff_psum = ctx.enter_context(tc.psum_pool(name="diff", bufs=2))
 
         loaded = {}
         grouped = {}
@@ -79,10 +81,13 @@ def tile_updatespeaker_pc_t_kernel(
         blend = {}
         diff = {}
 
+        def load(name, a):
+            loaded[(name, a)] = inputs.tile([P, PAIR, K], BF16, name="%s_%d" % (name, a), tag=name)
+            nc.sync.dma_start(out=loaded[(name, a)][:], in_=sources[name][:, PAIR * a : PAIR * (a + 1), :])
+
         def load_pair(a):
             for name in LOADED:
-                loaded[(name, a)] = inputs.tile([P, PAIR, K], BF16, name="%s_%d" % (name, a), tag=name)
-                nc.sync.dma_start(out=loaded[(name, a)][:], in_=sources[name][:, PAIR * a : PAIR * (a + 1), :])
+                load(name, a)
 
         def load_weight_scales(i):
             for q in range(P // QUADRANT):
@@ -97,69 +102,68 @@ def tile_updatespeaker_pc_t_kernel(
                 in_=weight_words[i][0].rearrange("p n t -> p (n t)").bitcast(I32),
             )
 
-        def transpose_tile(j):
-            a, s = divmod(j, PAIR)
-            if s == 0:
-                grouped[a] = grouped_pool.tile(
-                    [P, len(QUANTISED), PAIR, P, PACK], BF16, name="grouped_%d" % a, tag="grouped", align_bytes=64
+        def transpose_pair(a):
+            for i in (1, 0, 2):
+                name = QUANTISED[i]
+                bank = planes_psum.tile([P, PAIR, HALVES, P], F32, name="planes_%d_%d" % (a, i), tag="planes")
+                for s in range(PAIR):
+                    words = loaded[(name, a)][:, s, :].bitcast(F32)
+                    for u in range(HALVES):
+                        nc.tensor.transpose(bank[:, s, u, :], words[:, u : K // 2 : HALVES], identity[:])
+                grouped[(a, i)] = grouped_pool.tile(
+                    [P, PAIR, P, PACK], BF16, name="grouped_%d_%d" % (a, i), tag="grouped_%d" % i, align_bytes=64
                 )
-            two = planes_psum.tile([P, 2, HALVES, P], F32, name="two_%d" % j, tag="two")
-            one = planes_psum.tile([P, 1, HALVES, P], F32, name="one_%d" % j, tag="one")
-            for i, name in enumerate(QUANTISED):
-                words = loaded[(name, a)][:, s, :].bitcast(F32)
-                bank = two[:, i] if i < 2 else one[:, 0]
-                for u in range(HALVES):
-                    nc.tensor.transpose(bank[:, u, :], words[:, u : K // 2 : HALVES], identity[:])
-            as_words = grouped[a][:].bitcast(F32)
-            nc.scalar.copy(out=as_words[:, 0:2, s], in_=two[:].rearrange("p i u r -> p i r u"))
-            nc.scalar.copy(out=as_words[:, 2:3, s], in_=one[:].rearrange("p i u r -> p i r u"))
+                as_words = grouped[(a, i)][:].bitcast(F32)
+                nc.scalar.copy(out=as_words, in_=bank[:].rearrange("p s u r -> p s r u"))
 
-        def quantise_pair(a):
-            codes[a] = code_pool.tile([P, len(QUANTISED), PAIR * P], U32, name="codes_%d" % a, tag="codes", align_bytes=64)
-            scales[a] = code_pool.tile([P, len(QUANTISED), PAIR * P], U8, name="scales_%d" % a, tag="scales", align_bytes=64)
-            for some in (slice(0, 2), slice(2, 3)):
-                nc.vector.quantize_mx(
-                    out=codes[a][:, some, :].rearrange("p i w -> p (i w)").bitcast(FP8X4),
-                    scales=scales[a][:, some, :].rearrange("p i w -> p (i w)"),
-                    in_=grouped[a][:, some].rearrange("p i s r t -> p (i s r t)"),
-                )
+        def quantise(a, i):
+            codes[(a, i)] = code_pool.tile([P, PAIR * P], U32, name="codes_%d_%d" % (a, i), tag="codes_%d" % i, align_bytes=64)
+            scales[(a, i)] = code_pool.tile([P, PAIR * P], U8, name="scales_%d_%d" % (a, i), tag="scales_%d" % i, align_bytes=64)
+            nc.vector.quantize_mx(
+                out=codes[(a, i)][:].bitcast(FP8X4),
+                scales=scales[(a, i)][:],
+                in_=grouped[(a, i)][:].rearrange("p s r t -> p (s r t)"),
+            )
 
-        def multiply_tile(j):
-            a, s = divmod(j, PAIR)
-            if s == 0:
-                gate[a] = gate_pool.tile([P, PAIR, N], F32, name="gate_%d" % a, tag="gate")
-            rows = slice(s * P, (s + 1) * P)
-            sums = sums_psum.tile([P, N], F32, name="sums_%d" % j, tag="sums")
-            for i in range(len(QUANTISED)):
-                nc.tensor.matmul_mx(
-                    out=sums[:],
-                    lhsT=codes[a][:, i, rows].bitcast(FP8X4),
-                    lhsT_scale=scales[a][:, i, rows],
-                    rhs=w_words[:, i, :].bitcast(FP8X4),
-                    rhs_scale=w_scales[:, i, :],
-                    start=(i == 0),
-                    stop=(i == len(QUANTISED) - 1),
-                )
-            nc.scalar.activation(out=gate[a][:, s, :], in_=sums[:], func=ACT.Sigmoid)
-            if by_tensor(j):
-                diff[j] = diff_psum.tile([P, N], F32, name="diff_%d" % j, tag="diff")
-                nc.tensor.matmul(out=diff[j][:], lhsT=plus_identity[:], rhs=loaded[("ht", a)][:, s, :], start=True, stop=False)
-                nc.tensor.matmul(out=diff[j][:], lhsT=minus_identity[:], rhs=loaded[("hs", a)][:, s, :], start=False, stop=True)
+        def multiply_pair(a):
+            gate[a] = gate_pool.tile([P, PAIR, N], F32, name="gate_%d" % a, tag="gate")
+            for s in range(PAIR):
+                rows = slice(s * P, (s + 1) * P)
+                sums = sums_psum.tile([P, N], F32, name="sums_%d_%d" % (a, s), tag="sums")
+                for i in (1, 0, 2):
+                    nc.tensor.matmul_mx(
+                        out=sums[:],
+                        lhsT=codes[(a, i)][:, rows].bitcast(FP8X4),
+                        lhsT_scale=scales[(a, i)][:, rows],
+                        rhs=w_words[:, i, :].bitcast(FP8X4),
+                        rhs_scale=w_scales[:, i, :],
+                        start=(i == 1),
+                        stop=(i == 2),
+                    )
+                nc.scalar.activation(out=gate[a][:, s, :], in_=sums[:], func=ACT.Sigmoid)
 
         def by_tensor(j):
-            return j % TENSOR_SHARE == TENSOR_SHARE - 1
+            return j % TENSOR_PERIOD in TENSOR_TILES
 
-        def difference(j):
-            a, s = divmod(j, PAIR)
-            if s == 0:
-                blend[a] = blend_pool.tile([P, PAIR, N], F32, name="blend_%d" % a, tag="blend")
-            if not by_tensor(j):
-                nc.vector.tensor_tensor(
-                    out=blend[a][:, s, :], in0=loaded[("ht", a)][:, s, :], in1=loaded[("hs", a)][:, s, :], op=ALU.subtract
-                )
+        def difference(a):
+            blend[a] = blend_pool.tile([P, PAIR, N], F32, name="blend_%d" % a, tag="blend")
+            for s in range(PAIR):
+                j = PAIR * a + s
+                if not by_tensor(j):
+                    nc.vector.tensor_tensor(
+                        out=blend[a][:, s, :], in0=loaded[("ht", a)][:, s, :], in1=loaded[("hs", a)][:, s, :], op=ALU.subtract
+                    )
 
-        def apply_gate(j):
-            a, s = divmod(j, PAIR)
+        def tensor_difference(a):
+            for s in range(PAIR):
+                j = PAIR * a + s
+                if by_tensor(j):
+                    diff[j] = diff_psum.tile([P, N], F32, name="diff_%d" % j, tag="diff")
+                    nc.tensor.matmul(out=diff[j][:], lhsT=plus_identity[:], rhs=loaded[("ht", a)][:, s, :], start=True, stop=False)
+                    nc.tensor.matmul(out=diff[j][:], lhsT=minus_identity[:], rhs=loaded[("hs", a)][:, s, :], start=False, stop=True)
+
+        def apply_gate(a, s):
+            j = PAIR * a + s
             nc.vector.tensor_tensor(
                 out=blend[a][:, s, :],
                 in0=diff[j][:] if by_tensor(j) else blend[a][:, s, :],
@@ -167,10 +171,9 @@ def tile_updatespeaker_pc_t_kernel(
                 op=ALU.mult,
             )
 
-        def add_speaker_and_store(j):
-            a, s = divmod(j, PAIR)
+        def add_speaker_and_store(a, s):
             nc.vector.tensor_tensor(out=blend[a][:, s, :], in0=blend[a][:, s, :], in1=loaded[("hs", a)][:, s, :], op=ALU.add)
-            nc.sync.dma_start(out=out_tiles[:, j, :], in_=blend[a][:, s, :])
+            nc.sync.dma_start(out=out_tiles[:, PAIR * a + s, :], in_=blend[a][:, s, :])
 
         w_words = consts.tile([P, len(QUANTISED), N], U32, align_bytes=64)
         w_scales = consts.tile([P, len(QUANTISED), N], U8, align_bytes=64)
@@ -185,29 +188,45 @@ def tile_updatespeaker_pc_t_kernel(
         make_identity(nc, plus_identity[:])
         nc.vector.tensor_scalar_mul(out=minus_identity[:], in0=plus_identity[:], scalar1=-1.0)
 
-        load_pair(0)
+        load("hs", 0)
+        load("x", 0)
+        load("ha", 0)
+        load("ht", 0)
         load_weight_scales(0)
-        load_pair(1)
+        load("hs", 1)
+        load("x", 1)
+        load("ha", 1)
         load_weight_scales(1)
-        for i in range(len(QUANTISED)):
-            load_weight_words(i)
+        load_weight_words(0)
+        load_weight_words(1)
+        load_weight_words(2)
         load_weight_scales(2)
-        for a in range(2, LOAD_AHEAD):
-            load_pair(a)
+        load("ht", 1)
+        load_pair(2)
+        load_pair(3)
 
-        for j in range(N_TILES + BLEND_LAG):
-            a, s = divmod(j, PAIR)
-            if s == 0 and a + LOAD_AHEAD < N_PAIRS:
+        for a in range(N_PAIRS + BLEND_LAG):
+            if a + LOAD_AHEAD < N_PAIRS:
                 load_pair(a + LOAD_AHEAD)
-            if j < N_TILES:
-                transpose_tile(j)
-            if MX_LAG <= j < N_TILES + MX_LAG:
-                multiply_tile(j - MX_LAG)
-            if j >= BLEND_LAG:
-                apply_gate(j - BLEND_LAG)
-            if j < N_TILES:
-                difference(j)
-            if j < N_TILES and s == 1:
-                quantise_pair(a)
-            if j >= BLEND_LAG:
-                add_speaker_and_store(j - BLEND_LAG)
+            if a < N_PAIRS:
+                transpose_pair(a)
+            if MX_LAG <= a < N_PAIRS + MX_LAG:
+                tensor_difference(a - MX_LAG)
+                multiply_pair(a - MX_LAG)
+            blended = a - BLEND_LAG
+            if blended >= 0:
+                apply_gate(blended, 0)
+            if blended >= 0:
+                apply_gate(blended, 1)
+            if a + 0 < N_PAIRS:
+                difference(a + 0)
+            if a < N_PAIRS:
+                quantise(a, 1)
+            if blended >= 0:
+                add_speaker_and_store(blended, 0)
+            if a < N_PAIRS:
+                quantise(a, 0)
+            if blended >= 0:
+                add_speaker_and_store(blended, 1)
+            if a < N_PAIRS:
+                quantise(a, 2)

@@ -29,8 +29,8 @@ QUADRANT = 32
 LOAD_AHEAD = 4
 MX_LAG = 1
 BLEND_LAG = 2
-TENSOR_TILES = (1, 3, 5)
-TENSOR_PERIOD = 8
+TENSOR_TILES = (1, 3, 5, 7, 9, 11, 13, 15, 17, 19, 21, 23, 25, 27, 29, 31,)
+GP_TILES = ()
 
 FLOPS = 2 * ROWS * K * N * len(QUANTISED)
 
@@ -69,6 +69,7 @@ def tile_updatespeaker_pc_t_kernel(
         code_pool = ctx.enter_context(tc.tile_pool(name="codes", bufs=3))
         gate_pool = ctx.enter_context(tc.tile_pool(name="gate", bufs=3))
         blend_pool = ctx.enter_context(tc.tile_pool(name="blend", bufs=6))
+        sorted_pool = ctx.enter_context(tc.tile_pool(name="sorted", bufs=2))
         planes_psum = ctx.enter_context(tc.psum_pool(name="planes", bufs=4))
         sums_psum = ctx.enter_context(tc.psum_pool(name="sums", bufs=2))
         diff_psum = ctx.enter_context(tc.psum_pool(name="diff", bufs=2))
@@ -77,6 +78,7 @@ def tile_updatespeaker_pc_t_kernel(
         grouped = {}
         codes = {}
         scales = {}
+        ordered = {}
         gate = {}
         blend = {}
         diff = {}
@@ -102,6 +104,11 @@ def tile_updatespeaker_pc_t_kernel(
                 in_=weight_words[i][0].rearrange("p n t -> p (n t)").bitcast(I32),
             )
 
+        def sort_words(a, i):
+            name = QUANTISED[i]
+            ordered[(a, i)] = sorted_pool.tile([P, PAIR, HALVES, P], F32, name="sorted_%d_%d" % (a, i), tag="sorted_%d" % i)
+            nc.scalar.copy(out=ordered[(a, i)][:], in_=loaded[(name, a)][:].bitcast(F32).rearrange("p s (w u) -> p s u w", u=HALVES))
+
         def transpose_pair(a):
             for i in (1, 0, 2):
                 name = QUANTISED[i]
@@ -109,7 +116,7 @@ def tile_updatespeaker_pc_t_kernel(
                 for s in range(PAIR):
                     words = loaded[(name, a)][:, s, :].bitcast(F32)
                     for u in range(HALVES):
-                        nc.tensor.transpose(bank[:, s, u, :], words[:, u : K // 2 : HALVES], identity[:])
+                        nc.tensor.transpose(bank[:, s, u, :], ordered[(a, i)][:, s, u, :] if (a, i) in ordered else words[:, u : K // 2 : HALVES], identity[:])
                 grouped[(a, i)] = grouped_pool.tile(
                     [P, PAIR, P, PACK], BF16, name="grouped_%d_%d" % (a, i), tag="grouped_%d" % i, align_bytes=64
                 )
@@ -143,16 +150,19 @@ def tile_updatespeaker_pc_t_kernel(
                 nc.scalar.activation(out=gate[a][:, s, :], in_=sums[:], func=ACT.Sigmoid)
 
         def by_tensor(j):
-            return j % TENSOR_PERIOD in TENSOR_TILES
+            return j in TENSOR_TILES
 
         def difference(a):
             blend[a] = blend_pool.tile([P, PAIR, N], F32, name="blend_%d" % a, tag="blend")
-            for s in range(PAIR):
-                j = PAIR * a + s
-                if not by_tensor(j):
-                    nc.vector.tensor_tensor(
-                        out=blend[a][:, s, :], in0=loaded[("ht", a)][:, s, :], in1=loaded[("hs", a)][:, s, :], op=ALU.subtract
-                    )
+            mine = [s for s in range(PAIR) if not by_tensor(PAIR * a + s)]
+            if False and len(mine) == PAIR and PAIR * a not in GP_TILES:
+                nc.vector.tensor_tensor(out=blend[a][:], in0=loaded[("ht", a)][:], in1=loaded[("hs", a)][:], op=ALU.subtract)
+                return
+            for s in mine:
+                engine = nc.gpsimd if PAIR * a + s in GP_TILES else nc.vector
+                engine.tensor_tensor(
+                    out=blend[a][:, s, :], in0=loaded[("ht", a)][:, s, :], in1=loaded[("hs", a)][:, s, :], op=ALU.subtract
+                )
 
         def tensor_difference(a):
             for s in range(PAIR):
@@ -164,6 +174,10 @@ def tile_updatespeaker_pc_t_kernel(
 
         def apply_gate(a, s):
             j = PAIR * a + s
+            if False and not by_tensor(PAIR * a) and not by_tensor(PAIR * a + 1):
+                if s == 0:
+                    nc.vector.tensor_tensor(out=blend[a][:], in0=blend[a][:], in1=gate[a][:], op=ALU.mult)
+                return
             nc.vector.tensor_tensor(
                 out=blend[a][:, s, :],
                 in0=diff[j][:] if by_tensor(j) else blend[a][:, s, :],
@@ -172,6 +186,11 @@ def tile_updatespeaker_pc_t_kernel(
             )
 
         def add_speaker_and_store(a, s):
+            if False:
+                if s == 0:
+                    nc.vector.tensor_tensor(out=blend[a][:], in0=blend[a][:], in1=loaded[("hs", a)][:], op=ALU.add)
+                    nc.sync.dma_start(out=out_tiles[:, PAIR * a : PAIR * (a + 1), :], in_=blend[a][:])
+                return
             nc.vector.tensor_tensor(out=blend[a][:, s, :], in0=blend[a][:, s, :], in1=loaded[("hs", a)][:, s, :], op=ALU.add)
             nc.sync.dma_start(out=out_tiles[:, PAIR * a + s, :], in_=blend[a][:, s, :])
 
@@ -210,6 +229,9 @@ def tile_updatespeaker_pc_t_kernel(
                 load_pair(a + LOAD_AHEAD)
             if a < N_PAIRS:
                 transpose_pair(a)
+            for i in (1, 0, 2):
+                if a + 1 < N_PAIRS and ((a + i) % 2 == 0):
+                    sort_words(a + 1, i)
             if MX_LAG <= a < N_PAIRS + MX_LAG:
                 tensor_difference(a - MX_LAG)
                 multiply_pair(a - MX_LAG)

from contextlib import ExitStack

import concourse.mybir as mybir
from concourse.masks import make_identity

F32 = mybir.dt.float32
BF16 = mybir.dt.bfloat16
I32 = mybir.dt.int32
U32 = mybir.dt.uint32
U8 = mybir.dt.uint8
FP8X4 = mybir.dt.float8_e4m3fn_x4
ALU = mybir.AluOpType
ACT = mybir.ActivationFunctionType

P = 128
PACK = 4
HALVES = 2
ROWS = 4096
K = 512
N = 512
N_TILES = ROWS // P
PAIR = 2
N_PAIRS = N_TILES // PAIR
QUANTISED = ("x", "hs", "ha")
LOADED = ("hs", "x", "ha", "ht")
SCALE_ROWS = 4
QUADRANT = 32

LOAD_AHEAD = 4
MX_LAG = 1
BLEND_LAG = 2
TENSOR_TILES = (1, 3, 5, 7, 9, 11, 13, 15, 17, 19, 21, 23, 25, 27, 29, 31,)
GP_TILES = ()

FLOPS = 2 * ROWS * K * N * len(QUANTISED)


def tile_updatespeaker_pc_t_kernel(
    tc,
    encoder_hidden,
    spk_vectors,
    adr_vectors,
    h_tilde,
    WA_xz_words,
    WA_xz_scales,
    WA_hz_words,
    WA_hz_scales,
    VA_hz_words,
    VA_hz_scales,
    out,
):
    nc = tc.nc
    by_tile = "(p j) c -> p j c"
    sources = {
        "x": encoder_hidden.rearrange(by_tile, j=N_TILES),
        "hs": spk_vectors.rearrange(by_tile, j=N_TILES),
        "ha": adr_vectors.rearrange(by_tile, j=N_TILES),
        "ht": h_tilde.rearrange(by_tile, j=N_TILES),
    }
    out_tiles = out.rearrange(by_tile, j=N_TILES)
    weight_words = (WA_xz_words, WA_hz_words, VA_hz_words)
    weight_scales = (WA_xz_scales, WA_hz_scales, VA_hz_scales)

    with ExitStack() as ctx:
        ctx.enter_context(tc.manual_schedule())
        consts = ctx.enter_context(tc.tile_pool(name="consts", bufs=1))
        inputs = ctx.enter_context(tc.tile_pool(name="inputs", bufs=N_PAIRS))
        grouped_pool = ctx.enter_context(tc.tile_pool(name="grouped", bufs=3))
        code_pool = ctx.enter_context(tc.tile_pool(name="codes", bufs=3))
        gate_pool = ctx.enter_context(tc.tile_pool(name="gate", bufs=3))
        blend_pool = ctx.enter_context(tc.tile_pool(name="blend", bufs=6))
        sorted_pool = ctx.enter_context(tc.tile_pool(name="sorted", bufs=2))
        planes_psum = ctx.enter_context(tc.psum_pool(name="planes", bufs=4))
        sums_psum = ctx.enter_context(tc.psum_pool(name="sums", bufs=2))
        diff_psum = ctx.enter_context(tc.psum_pool(name="diff", bufs=2))

        loaded = {}
        grouped = {}
        codes = {}
        scales = {}
        ordered = {}
        gate = {}
        blend = {}
        diff = {}

        def load(name, a):
            loaded[(name, a)] = inputs.tile([P, PAIR, K], BF16, name="%s_%d" % (name, a), tag=name)
            nc.sync.dma_start(out=loaded[(name, a)][:], in_=sources[name][:, PAIR * a : PAIR * (a + 1), :])

        def load_pair(a):
            for name in LOADED:
                load(name, a)

        def load_weight_scales(i):
            for q in range(P // QUADRANT):
                nc.sync.dma_start(
                    out=w_scales[QUADRANT * q : QUADRANT * q + SCALE_ROWS, i, :].bitcast(I32),
                    in_=weight_scales[i][0, SCALE_ROWS * q : SCALE_ROWS * (q + 1), :].bitcast(I32),
                )

        def load_weight_words(i):
            nc.sync.dma_start(
                out=w_words[:, i, :].bitcast(I32),
                in_=weight_words[i][0].rearrange("p n t -> p (n t)").bitcast(I32),
            )

        def sort_words(a, i):
            name = QUANTISED[i]
            ordered[(a, i)] = sorted_pool.tile([P, PAIR, HALVES, P], F32, name="sorted_%d_%d" % (a, i), tag="sorted_%d" % i)
            nc.scalar.copy(out=ordered[(a, i)][:], in_=loaded[(name, a)][:].bitcast(F32).rearrange("p s (w u) -> p s u w", u=HALVES))

        def transpose_pair(a):
            for i in (1, 0, 2):
                name = QUANTISED[i]
                bank = planes_psum.tile([P, PAIR, HALVES, P], F32, name="planes_%d_%d" % (a, i), tag="planes")
                for s in range(PAIR):
                    words = loaded[(name, a)][:, s, :].bitcast(F32)
                    for u in range(HALVES):
                        nc.tensor.transpose(bank[:, s, u, :], ordered[(a, i)][:, s, u, :] if (a, i) in ordered else words[:, u : K // 2 : HALVES], identity[:])
                grouped[(a, i)] = grouped_pool.tile(
                    [P, PAIR, P, PACK], BF16, name="grouped_%d_%d" % (a, i), tag="grouped_%d" % i, align_bytes=64
                )
                as_words = grouped[(a, i)][:].bitcast(F32)
                nc.scalar.copy(out=as_words, in_=bank[:].rearrange("p s u r -> p s r u"))

        def quantise(a, i):
            codes[(a, i)] = code_pool.tile([P, PAIR * P], U32, name="codes_%d_%d" % (a, i), tag="codes_%d" % i, align_bytes=64)
            scales[(a, i)] = code_pool.tile([P, PAIR * P], U8, name="scales_%d_%d" % (a, i), tag="scales_%d" % i, align_bytes=64)
            nc.vector.quantize_mx(
                out=codes[(a, i)][:].bitcast(FP8X4),
                scales=scales[(a, i)][:],
                in_=grouped[(a, i)][:].rearrange("p s r t -> p (s r t)"),
            )

        def multiply_pair(a):
            gate[a] = gate_pool.tile([P, PAIR, N], F32, name="gate_%d" % a, tag="gate")
            for s in range(PAIR):
                rows = slice(s * P, (s + 1) * P)
                sums = sums_psum.tile([P, N], F32, name="sums_%d_%d" % (a, s), tag="sums")
                for i in (1, 0, 2):
                    nc.tensor.matmul_mx(
                        out=sums[:],
                        lhsT=codes[(a, i)][:, rows].bitcast(FP8X4),
                        lhsT_scale=scales[(a, i)][:, rows],
                        rhs=w_words[:, i, :].bitcast(FP8X4),
                        rhs_scale=w_scales[:, i, :],
                        start=(i == 1),
                        stop=(i == 2),
                    )
                nc.scalar.activation(out=gate[a][:, s, :], in_=sums[:], func=ACT.Sigmoid)

        def by_tensor(j):
            return j in TENSOR_TILES

        def difference(a):
            blend[a] = blend_pool.tile([P, PAIR, N], F32, name="blend_%d" % a, tag="blend")
            mine = [s for s in range(PAIR) if not by_tensor(PAIR * a + s)]
            if False and len(mine) == PAIR and PAIR * a not in GP_TILES:
                nc.vector.tensor_tensor(out=blend[a][:], in0=loaded[("ht", a)][:], in1=loaded[("hs", a)][:], op=ALU.subtract)
                return
            for s in mine:
                engine = nc.gpsimd if PAIR * a + s in GP_TILES else nc.vector
                engine.tensor_tensor(
                    out=blend[a][:, s, :], in0=loaded[("ht", a)][:, s, :], in1=loaded[("hs", a)][:, s, :], op=ALU.subtract
                )

        def tensor_difference(a):
            for s in range(PAIR):
                j = PAIR * a + s
                if by_tensor(j):
                    diff[j] = diff_psum.tile([P, N], F32, name="diff_%d" % j, tag="diff")
                    nc.tensor.matmul(out=diff[j][:], lhsT=plus_identity[:], rhs=loaded[("ht", a)][:, s, :], start=True, stop=False)
                    nc.tensor.matmul(out=diff[j][:], lhsT=minus_identity[:], rhs=loaded[("hs", a)][:, s, :], start=False, stop=True)

        def apply_gate(a, s):
            j = PAIR * a + s
            if False and not by_tensor(PAIR * a) and not by_tensor(PAIR * a + 1):
                if s == 0:
                    nc.vector.tensor_tensor(out=blend[a][:], in0=blend[a][:], in1=gate[a][:], op=ALU.mult)
                return
            nc.vector.tensor_tensor(
                out=blend[a][:, s, :],
                in0=diff[j][:] if by_tensor(j) else blend[a][:, s, :],
                in1=gate[a][:, s, :],
                op=ALU.mult,
            )

        def add_speaker_and_store(a, s):
            if False:
                if s == 0:
                    nc.vector.tensor_tensor(out=blend[a][:], in0=blend[a][:], in1=loaded[("hs", a)][:], op=ALU.add)
                    nc.sync.dma_start(out=out_tiles[:, PAIR * a : PAIR * (a + 1), :], in_=blend[a][:])
                return
            nc.vector.tensor_tensor(out=blend[a][:, s, :], in0=blend[a][:, s, :], in1=loaded[("hs", a)][:, s, :], op=ALU.add)
            nc.sync.dma_start(out=out_tiles[:, PAIR * a + s, :], in_=blend[a][:, s, :])

        w_words = consts.tile([P, len(QUANTISED), N], U32, align_bytes=64)
        w_scales = consts.tile([P, len(QUANTISED), N], U8, align_bytes=64)
        identity = consts.tile([P, P], F32)
        warm = consts.tile([P, 1], F32)
        nc.vector.memset(w_scales[:].bitcast(I32), 0)
        nc.vector.memset(warm[:], 0.0)
        nc.scalar.activation(out=warm[:], in_=warm[:], func=ACT.Sigmoid)
        make_identity(nc, identity[:])
        plus_identity = consts.tile([P, P], BF16)
        minus_identity = consts.tile([P, P], BF16)
        make_identity(nc, plus_identity[:])
        nc.vector.tensor_scalar_mul(out=minus_identity[:], in0=plus_identity[:], scalar1=-1.0)

        load("hs", 0)
        load("x", 0)
        load("ha", 0)
        load("ht", 0)
        load_weight_scales(0)
        load("hs", 1)
        load("x", 1)
        load("ha", 1)
        load_weight_scales(1)
        load_weight_words(0)
        load_weight_words(1)
        load_weight_words(2)
        load_weight_scales(2)
        load("ht", 1)
        load_pair(2)
        load_pair(3)

        for a in range(N_PAIRS + BLEND_LAG):
            if a + LOAD_AHEAD < N_PAIRS:
                load_pair(a + LOAD_AHEAD)
            if a < N_PAIRS:
                transpose_pair(a)
            for i in (1, 0, 2):
                if a + 1 < N_PAIRS and ((a + i) % 2 == 0):
                    sort_words(a + 1, i)
            if MX_LAG <= a < N_PAIRS + MX_LAG:
                tensor_difference(a - MX_LAG)
                multiply_pair(a - MX_LAG)
            blended = a - BLEND_LAG
            if blended >= 0:
                apply_gate(blended, 0)
            if blended >= 0:
                apply_gate(blended, 1)
            if a + 0 < N_PAIRS:
                difference(a + 0)
            if a < N_PAIRS:
                quantise(a, 1)
            if blended >= 0:
                add_speaker_and_store(blended, 0)
            if a < N_PAIRS:
                quantise(a, 0)
            if blended >= 0:
                add_speaker_and_store(blended, 1)
            if a < N_PAIRS:
                quantise(a, 2)
